import numpy as np
import ml_dtypes


def mxq(x, axis, fmt="e4m3"):
    dtype, down = {"e4m3": (ml_dtypes.float8_e4m3fn, 7), "e5m2": (ml_dtypes.float8_e5m2, 14)}[fmt]
    v = np.moveaxis(np.asarray(x, np.float32).astype(ml_dtypes.bfloat16).astype(np.float64), axis, -1)
    blocks = v.reshape(v.shape[:-1] + (-1, 32))
    amax = np.abs(blocks).max(-1, keepdims=True)
    byte = np.maximum(np.where(amax > 0, np.frexp(amax)[1] - 1 + 127, 0) - down, 1)
    scale = np.exp2(byte - 127.0)
    codes = (blocks / scale).astype(np.float32).astype(dtype).astype(np.float64)
    return np.moveaxis((codes * scale).reshape(v.shape), -1, axis)


WIDE = False


def mx_kscale(k):
    if not WIDE:
        return np.ones(k)
    levels = np.array([10, -10, 5, -5, 0])
    a = np.random.permutation(np.resize(levels, k // 512 * 4)).reshape(k // 512, 4)
    idx = np.arange(k)
    return np.exp2(a[idx // 512, idx % 128 // 32])


BF16 = ml_dtypes.bfloat16


def bf(x):
    return np.asarray(x, np.float32).astype(BF16)


def f64(x):
    return np.asarray(x).astype(np.float64)


B, D, E, NM = 8192, 512, 128, 4


def setup_inputs():
    s, t = mx_kscale(D), mx_kscale(D)
    gain = np.ones((E, NM))
    gain[:, 1] = 0.3
    off = np.zeros((E, NM))
    off[:, 1] = 1.3 * np.sign(np.random.standard_normal(E))
    return {
        "prev_act": bf(np.maximum(np.random.standard_normal((B, D)) * 1.2, 0.0) * s),
        "W1": bf(np.random.standard_normal((D, D)) / np.sqrt(D) / s[:, None] * t),
        "b1": bf(np.random.standard_normal(D) * 0.2 * t),
        "W2": bf(np.random.standard_normal((D, NM * E)) / np.sqrt(D) * gain.reshape(-1) / t[:, None]),
        "b2": bf(np.random.standard_normal(NM * E) * 0.1 + off.reshape(-1)),
        "dopamine": bf(np.random.standard_normal((B, E))),
        "serotonin": bf(np.random.standard_normal((B, E))),
        "glutamate": bf(np.random.standard_normal((B, E))),
        "gaba": bf(np.random.standard_normal((B, E))),
    }


def reference(prev_act, W1, b1, W2, b2, dopamine, serotonin, glutamate, gaba):
    hid = np.maximum((mxq(f64(prev_act), 1, "e4m3") @ mxq(f64(W1), 0, "e4m3")) + f64(b1), 0.0)
    h = np.tanh((mxq(hid, 1, "e4m3") @ mxq(f64(W2), 0, "e4m3")) + f64(b2))
    preds = h.reshape(B, E, NM)
    p_dop, p_ser, p_glu, p_gab = preds[..., 0], preds[..., 1], preds[..., 2], preds[..., 3]
    inv = 1.0 / np.maximum(np.abs(p_ser), 1e-6)
    dop = f64(dopamine) + p_dop * inv
    ser = f64(serotonin) + p_ser
    glu = f64(glutamate) + p_glu * inv
    gab = f64(gaba) + p_gab * inv
    return np.concatenate([dop, ser, glu, gab], axis=0)

@@ -1,0 +1,332 @@
+from contextlib import ExitStack
+
+import concourse.mybir as mybir
+from concourse.masks import make_identity
+
+F32 = mybir.dt.float32
+BF16 = mybir.dt.bfloat16
+U32 = mybir.dt.uint32
+U8 = mybir.dt.uint8
+FP8X4 = mybir.dt.float8_e4m3fn_x4
+ACT = mybir.ActivationFunctionType
+ALU = mybir.AluOpType
+
+P = 128
+B, D, E, NM = 8192, 512, 128, 4
+FLOPS = 2 * B * D * D + 2 * B * D * NM * E
+NT = B // P
+SCT = 4
+W = SCT * P
+NSC = NT // SCT
+XTA = 8
+MTA = 8
+GROUP = 4
+LAG = 5
+SER = 1
+OTHERS = [0, 2, 3]
+G_PLANES = 0
+
+
+def tile_hebbianlayer_pb_t_kernel(
+    tc, prev_act, W1, b1, W2, b2, dopamine, serotonin, glutamate, gaba, out
+):
+    nc = tc.nc
+    x_view = prev_act.rearrange("(p a) k -> p (a k)", a=NT)
+    mod_views = [
+        m.rearrange("(p a) j -> p a j", a=NT)
+        for m in (dopamine, serotonin, glutamate, gaba)
+    ]
+    out_view = out.rearrange("(c p a) j -> p c a j", c=NM, p=P, a=NT)
+
+    with ExitStack() as ctx:
+        const = ctx.enter_context(tc.tile_pool(name="const", bufs=1))
+        xin = ctx.enter_context(tc.tile_pool(name="xin", bufs=2))
+        work = ctx.enter_context(tc.tile_pool(name="work", bufs=3))
+        codes = ctx.enter_context(tc.tile_pool(name="codes", bufs=2))
+        hcodes = ctx.enter_context(tc.tile_pool(name="hcodes", bufs=8))
+        serp = ctx.enter_context(tc.tile_pool(name="serp", bufs=9))
+        post = ctx.enter_context(tc.tile_pool(name="post", bufs=3))
+        resp = ctx.enter_context(tc.tile_pool(name="resp", bufs=3))
+        modp = ctx.enter_context(tc.tile_pool(name="modp", bufs=3))
+        ps_xt = ctx.enter_context(tc.psum_pool(name="ps_xt", bufs=2))
+        ps_mm = ctx.enter_context(tc.psum_pool(name="ps_mm", bufs=4))
+        ps_ot = ctx.enter_context(tc.psum_pool(name="ps_ot", bufs=2))
+        ctx.enter_context(tc.manual_schedule())
+
+        x_tiles, gx_t, xt_t, xc_t, mm_t, hidp_t, gh_t, hc_t = {}, {}, {}, {}, {}, {}, {}, {}
+        ser_t, inv_t, ht_t, ot_t, res_t, mod_t = {}, {}, {}, {}, {}, {}
+
+        def live(i):
+            return 0 <= i < NSC
+
+        def load_x(g):
+            if g * XTA >= NT or g in x_tiles:
+                return
+            xr = xin.tile([P, XTA * D], BF16, name="xr")
+            nc.sync.dma_start(out=xr[:], in_=x_view[:, g * XTA * D : (g + 1) * XTA * D])
+            x_tiles[g] = xr
+
+        def load_mods(i):
+            g = i * SCT // MTA
+            if not live(i) or g in mod_t:
+                return
+            mt = modp.tile([P, NM, MTA, E], BF16, name="mt")
+            for c in range(NM):
+                nc.sync.dma_start(out=mt[:, c, :, :], in_=mod_views[c][:, g * MTA : (g + 1) * MTA, :])
+            mod_t[g] = mt
+
+        ident = const.tile([P, P], F32)
+        make_identity(nc, ident[:])
+        raw1 = const.tile([P, 4, D], BF16)
+        for u in range(2):
+            nc.sync.dma_start(
+                out=raw1[:, 2 * u : 2 * u + 2, :],
+                in_=W1[256 * u : 256 * u + 256, :].rearrange("(q e) f -> q e f", e=2),
+            )
+        load_x(0)
+        raw2 = const.tile([P, 4, D], BF16)
+        b1_bf = const.tile([P, 4], BF16)
+        b2_bf = const.tile([P, 4], BF16)
+        nc.scalar.dma_start(out=b1_bf[:], in_=b1.rearrange("(m t) -> m t", t=4))
+        nc.scalar.dma_start(out=raw2[:], in_=W2.rearrange("(p t) n -> p t n", t=4))
+        nc.scalar.dma_start(out=b2_bf[:], in_=b2.rearrange("(j c) -> j c", c=4))
+        load_x(1)
+
+        g1 = const.tile([P, D, 4], BF16, align_bytes=64)
+        w1c = const.tile([P, D], U32, align_bytes=64)
+        w1s = const.tile([P, D], U8, align_bytes=64)
+        nc.vector.tensor_copy(
+            out=g1[:].rearrange("q (t m) j -> q t m j", t=4),
+            in_=raw1[:].rearrange("q j (m t) -> q t m j", t=4),
+        )
+        nc.vector.quantize_mx(
+            out=w1c[:].bitcast(FP8X4), scales=w1s[:], in_=g1[:].rearrange("q c j -> q (c j)")
+        )
+        b1t = const.tile([P, 4], F32)
+        b2t = const.tile([P, 4], F32)
+        nc.vector.tensor_copy(out=b1t[:], in_=b1_bf[:])
+        g2 = const.tile([P, D, 4], BF16, align_bytes=64)
+        w2c = const.tile([P, D], U32, align_bytes=64)
+        w2s = const.tile([P, D], U8, align_bytes=64)
+        nc.scalar.copy(
+            out=g2[:].rearrange("q (c m) j -> q c m j", c=4),
+            in_=raw2[:].rearrange("q j (m c) -> q c m j", c=4),
+        )
+
+        def quantise_w2():
+            nc.vector.tensor_copy(out=b2t[:], in_=b2_bf[:])
+            nc.vector.quantize_mx(
+                out=w2c[:].bitcast(FP8X4), scales=w2s[:], in_=g2[:].rearrange("q c j -> q (c j)")
+            )
+
+        def transpose_x(i, h):
+            if not live(i):
+                return
+            g, off = divmod(i * SCT, XTA)
+            if off == 0 and h == 0:
+                load_x(g + 1)
+            x32 = x_tiles[g][:].bitcast(F32)
+            xt = ps_xt.tile([P, 2, 2, P], F32, name="xt")
+            for al in range(2):
+                for u in range(2):
+                    col = (off + 2 * h + al) * 256 + u * P
+                    nc.tensor.transpose(xt[:, al, u, :], x32[:, col : col + P], ident[:])
+            xt_t[(i, h)] = xt
+
+        def copy_x(i, h):
+            if not live(i):
+                return
+            if i not in gx_t:
+                gx = work.tile([P, 4 * W], BF16, align_bytes=64, name="gx")
+                gx_t[i] = gx
+            gx32 = gx_t[i][:].bitcast(F32).rearrange("q (a b u) -> q a b u", a=SCT, u=2)
+            src = xt_t[(i, h)][:].rearrange("q a u b -> q a b u")
+            if h == 0:
+                nc.scalar.copy(out=gx32[:, 2 * h : 2 * h + 2], in_=src)
+            else:
+                nc.vector.tensor_copy(out=gx32[:, 2 * h : 2 * h + 2], in_=src)
+
+        def quantise_x(i):
+            if not live(i):
+                return
+            xc = codes.tile([P, W], U32, align_bytes=64, name="xc")
+            xs = codes.tile([P, W], U8, align_bytes=64, name="xs")
+            nc.vector.quantize_mx(out=xc[:].bitcast(FP8X4), scales=xs[:], in_=gx_t[i][:])
+            xc_t[i] = (xc, xs)
+
+        def mx_pass(key, wc, ws, col, operand):
+            acc = ps_mm.tile([P, W], F32, name="mm")
+            nc.tensor.matmul_mx(
+                out=acc[:],
+                lhsT=wc[:, col * P : (col + 1) * P].bitcast(FP8X4),
+                lhsT_scale=ws[:, col * P : (col + 1) * P],
+                rhs=operand[0][:].bitcast(FP8X4),
+                rhs_scale=operand[1][:],
+                start=True,
+                stop=True,
+            )
+            mm_t[key] = acc
+
+        def layer1(i, t):
+            if live(i):
+                mx_pass((1, i, t), w1c, w1s, t, xc_t[i])
+
+        def relu(i, t):
+            if not live(i):
+                return
+            if i not in hidp_t:
+                hidp = work.tile([P, 4, W], BF16, name="hidp")
+                hidp_t[i] = hidp
+
+            nc.scalar.activation(
+                out=hidp_t[i][:, t, :], in_=mm_t[(1, i, t)][:], func=ACT.Relu, bias=b1t[:, t : t + 1], scale=1.0
+            )
+
+        def regroup_hid(i):
+            if not live(i):
+                return
+            gh = work.tile([P, W, 4], BF16, align_bytes=64, name="gh")
+            nc.vector.tensor_copy(
+                out=gh[:].rearrange("p (c i) t -> p c t i", i=4),
+                in_=hidp_t[i][:].rearrange("p t (c i) -> p c t i", i=4),
+            )
+            gh_t[i] = gh
+
+        def quantise_hid(i):
+            if not live(i):
+                return
+            hc = hcodes.tile([P, W], U32, align_bytes=64, name="hc")
+            hs = hcodes.tile([P, W], U8, align_bytes=64, name="hs")
+            nc.vector.quantize_mx(
+                out=hc[:].bitcast(FP8X4), scales=hs[:], in_=gh_t[i][:].rearrange("p w t -> p (w t)")
+            )
+            hc_t[i] = (hc, hs)
+
+        def layer2_ser(i):
+            if live(i):
+                mx_pass((2, i, SER), w2c, w2s, SER, hc_t[i])
+
+        def tanh_ser(i):
+            if not live(i):
+                return
+            ser = serp.tile([P, W], F32, name="ser")
+            nc.scalar.activation(
+                out=ser[:], in_=mm_t[(2, i, SER)][:], func=ACT.Tanh, bias=b2t[:, SER : SER + 1], scale=1.0
+            )
+            ser_t[i] = ser
+
+        def square_ser(i):
+            if not live(i):
+                return
+            inv = serp.tile([P, W], F32, name="inv")
+            nc.scalar.activation(out=inv[:], in_=ser_t[i][:], func=ACT.Square)
+            inv_t[i] = inv
+
+        def reciprocals(s):
+            last = s - 3
+            if live(last) and last % GROUP == GROUP - 1:
+                for i in range(last - GROUP + 1, last + 1):
+                    nc.scalar.activation(out=inv_t[i][:], in_=inv_t[i][:], func=ACT.Abs_reciprocal_sqrt)
+
+        def layer2(i, n):
+            if live(i):
+                mx_pass((2, i, OTHERS[n]), w2c, w2s, OTHERS[n], hc_t[i])
+
+        def tanh(i, n):
+            if not live(i):
+                return
+            if i not in ht_t:
+                ht = post.tile([P, 3, W], F32, name="ht")
+                ht_t[i] = ht
+            c = OTHERS[n]
+            nc.scalar.activation(
+                out=ht_t[i][:, n, :], in_=mm_t[(2, i, c)][:], func=ACT.Tanh, bias=b2t[:, c : c + 1], scale=1.0
+            )
+
+        def products(i):
+            if not live(i):
+                return
+            nv = 3 - G_PLANES
+            if G_PLANES > 0:
+                nc.gpsimd.tensor_scalar(
+                    out=inv_t[i][:], in0=inv_t[i][:], scalar1=1.0e6, scalar2=0.0, op0=ALU.min, op1=ALU.max
+                )
+                for n in range(nv, 3):
+                    nc.gpsimd.tensor_tensor(out=ht_t[i][:, n, :], in0=ht_t[i][:, n, :], in1=inv_t[i][:], op=ALU.mult)
+            if nv > 0:
+                nc.vector.scalar_tensor_tensor(
+                    out=ht_t[i][:, 0:nv, :],
+                    in0=inv_t[i][:].unsqueeze(1).to_broadcast([P, nv, W]),
+                    scalar=1.0e6,
+                    in1=ht_t[i][:, 0:nv, :],
+                    op0=ALU.min,
+                    op1=ALU.mult,
+                )
+
+        def transpose_back(i, al):
+            if not live(i):
+                return
+            ot = ps_ot.tile([P, NM, E], F32, name="ot")
+            for c in range(NM):
+                if c == SER:
+                    src = ser_t[i][:, al * P : (al + 1) * P]
+                else:
+                    src = ht_t[i][:, OTHERS.index(c), al * P : (al + 1) * P]
+                nc.tensor.transpose(ot[:, c, :], src, ident[:])
+            ot_t[(i, al)] = ot
+
+        def add_modulators(i, al):
+            if not live(i):
+                return
+            if i not in res_t:
+                res = resp.tile([P, NM, SCT, E], F32, name="res")
+                res_t[i] = res
+            g, off = divmod(i * SCT, MTA)
+            nc.vector.tensor_tensor(
+                out=res_t[i][:, :, al, :], in0=ot_t[(i, al)][:], in1=mod_t[g][:, :, off + al, :], op=ALU.add
+            )
+
+        def store(i):
+            if live(i):
+                nc.sync.dma_start(out=out_view[:, :, i * SCT : (i + 1) * SCT, :], in_=res_t[i][:])
+
+        for s in range(-1, NSC + LAG + 3 + 1):
+            j = s - LAG
+            load_mods(j + 1)
+            add_modulators(j - 2, 0)
+            copy_x(s, 0)
+            copy_x(s, 1)
+            square_ser(s - 3)
+            reciprocals(s)
+            add_modulators(j - 2, 1)
+            transpose_back(j - 2, 2)
+            transpose_back(j - 2, 3)
+            transpose_x(s + 1, 0)
+            layer2(j, 0)
+            layer2(j, 1)
+            layer2(j, 2)
+            layer2_ser(s - 2)
+            relu(s - 1, 0)
+            relu(s - 1, 1)
+            relu(s - 1, 2)
+            relu(s - 1, 3)
+            products(j - 1)
+            add_modulators(j - 2, 2)
+            quantise_x(s)
+            add_modulators(j - 2, 3)
+            store(j - 2)
+            tanh(j, 0)
+            tanh(j, 1)
+            tanh(j, 2)
+            tanh_ser(s - 2)
+            transpose_x(s + 1, 1)
+            transpose_back(j - 1, 0)
+            transpose_back(j - 1, 1)
+            layer1(s, 0)
+            layer1(s, 1)
+            layer1(s, 2)
+            layer1(s, 3)
+            regroup_hid(s - 1)
+            quantise_hid(s - 1)
+            if s == 0:
+                quantise_w2()

@@ -24,7 +24,7 @@ GROUP = 4
 LAG = 5
 SER = 1
 OTHERS = [0, 2, 3]
-G_PLANES = 0
+G_PLANES = 3
 
 
 def tile_hebbianlayer_pb_t_kernel(
@@ -44,8 +44,8 @@ def tile_hebbianlayer_pb_t_kernel(
         work = ctx.enter_context(tc.tile_pool(name="work", bufs=3))
         codes = ctx.enter_context(tc.tile_pool(name="codes", bufs=2))
         hcodes = ctx.enter_context(tc.tile_pool(name="hcodes", bufs=8))
-        serp = ctx.enter_context(tc.tile_pool(name="serp", bufs=9))
-        post = ctx.enter_context(tc.tile_pool(name="post", bufs=3))
+        serp = ctx.enter_context(tc.tile_pool(name="serp", bufs=10))
+        post = ctx.enter_context(tc.tile_pool(name="post", bufs=4))
         resp = ctx.enter_context(tc.tile_pool(name="resp", bufs=3))
         modp = ctx.enter_context(tc.tile_pool(name="modp", bufs=3))
         ps_xt = ctx.enter_context(tc.psum_pool(name="ps_xt", bufs=2))
@@ -141,7 +141,7 @@ def tile_hebbianlayer_pb_t_kernel(
                 gx_t[i] = gx
             gx32 = gx_t[i][:].bitcast(F32).rearrange("q (a b u) -> q a b u", a=SCT, u=2)
             src = xt_t[(i, h)][:].rearrange("q a u b -> q a b u")
-            if h == 0:
+            if False:
                 nc.scalar.copy(out=gx32[:, 2 * h : 2 * h + 2], in_=src)
             else:
                 nc.vector.tensor_copy(out=gx32[:, 2 * h : 2 * h + 2], in_=src)
@@ -177,7 +177,12 @@ def tile_hebbianlayer_pb_t_kernel(
             if i not in hidp_t:
                 hidp = work.tile([P, 4, W], BF16, name="hidp")
                 hidp_t[i] = hidp
-
+            if t == 3:
+                nc.vector.tensor_scalar(
+                    out=hidp_t[i][:, t, :], in0=mm_t[(1, i, t)][:], scalar1=b1t[:, t : t + 1], scalar2=0.0,
+                    op0=ALU.add, op1=ALU.max,
+                )
+                return
             nc.scalar.activation(
                 out=hidp_t[i][:, t, :], in_=mm_t[(1, i, t)][:], func=ACT.Relu, bias=b1t[:, t : t + 1], scale=1.0
             )
@@ -293,40 +298,40 @@ def tile_hebbianlayer_pb_t_kernel(
         for s in range(-1, NSC + LAG + 3 + 1):
             j = s - LAG
             load_mods(j + 1)
-            add_modulators(j - 2, 0)
-            copy_x(s, 0)
-            copy_x(s, 1)
             square_ser(s - 3)
+            transpose_back(j - 3, 2)
             reciprocals(s)
-            add_modulators(j - 2, 1)
-            transpose_back(j - 2, 2)
-            transpose_back(j - 2, 3)
-            transpose_x(s + 1, 0)
+            transpose_back(j - 3, 3)
             layer2(j, 0)
-            layer2(j, 1)
-            layer2(j, 2)
-            layer2_ser(s - 2)
-            relu(s - 1, 0)
-            relu(s - 1, 1)
             relu(s - 1, 2)
+            layer2_ser(s - 2)
+            add_modulators(j - 3, 1)
+            layer2(j, 1)
+            add_modulators(j - 3, 0)
+            relu(s - 1, 1)
+            copy_x(s, 1)
+            layer2(j, 2)
+            relu(s - 1, 0)
+            transpose_back(j - 2, 1)
             relu(s - 1, 3)
-            products(j - 1)
-            add_modulators(j - 2, 2)
-            quantise_x(s)
-            add_modulators(j - 2, 3)
-            store(j - 2)
+            transpose_x(s + 1, 0)
+            add_modulators(j - 3, 2)
             tanh(j, 0)
-            tanh(j, 1)
-            tanh(j, 2)
             tanh_ser(s - 2)
+            transpose_back(j - 2, 0)
+            tanh(j, 1)
+            products(j - 1)
+            add_modulators(j - 3, 3)
+            copy_x(s, 0)
+            store(j - 3)
             transpose_x(s + 1, 1)
-            transpose_back(j - 1, 0)
-            transpose_back(j - 1, 1)
-            layer1(s, 0)
-            layer1(s, 1)
+            quantise_x(s)
             layer1(s, 2)
-            layer1(s, 3)
             regroup_hid(s - 1)
+            tanh(j, 2)
             quantise_hid(s - 1)
+            layer1(s, 1)
+            layer1(s, 3)
+            layer1(s, 0)
             if s == 0:
                 quantise_w2()

@@ -18,13 +18,19 @@ NT = B // P
 SCT = 4
 W = SCT * P
 NSC = NT // SCT
-XTA = 8
-MTA = 8
-GROUP = 4
-LAG = 5
+PAIR = 2 * SCT
 SER = 1
 OTHERS = [0, 2, 3]
-G_PLANES = 3
+EARLY = 4
+MO_BUFS = 5
+
+
+def ser_on_scalar(i):
+    return i % 2 == 1
+
+
+def back_on_scalar(i, k):
+    return i >= EARLY and (k == 2 or (k == 1 and i % 2 == 0))
 
 
 def tile_hebbianlayer_pb_t_kernel(
@@ -32,51 +38,57 @@ def tile_hebbianlayer_pb_t_kernel(
 ):
     nc = tc.nc
     x_view = prev_act.rearrange("(p a) k -> p (a k)", a=NT)
-    mod_views = [
-        m.rearrange("(p a) j -> p a j", a=NT)
-        for m in (dopamine, serotonin, glutamate, gaba)
-    ]
+    ser_view = serotonin.rearrange("(p a) j -> p a j", a=NT)
+    other_views = [m.rearrange("(p a) j -> p a j", a=NT) for m in (dopamine, glutamate, gaba)]
     out_view = out.rearrange("(c p a) j -> p c a j", c=NM, p=P, a=NT)
 
     with ExitStack() as ctx:
         const = ctx.enter_context(tc.tile_pool(name="const", bufs=1))
         xin = ctx.enter_context(tc.tile_pool(name="xin", bufs=2))
-        work = ctx.enter_context(tc.tile_pool(name="work", bufs=3))
+        work = ctx.enter_context(tc.tile_pool(name="work", bufs=2))
         codes = ctx.enter_context(tc.tile_pool(name="codes", bufs=2))
-        hcodes = ctx.enter_context(tc.tile_pool(name="hcodes", bufs=8))
-        serp = ctx.enter_context(tc.tile_pool(name="serp", bufs=10))
-        post = ctx.enter_context(tc.tile_pool(name="post", bufs=4))
-        resp = ctx.enter_context(tc.tile_pool(name="resp", bufs=3))
-        modp = ctx.enter_context(tc.tile_pool(name="modp", bufs=3))
-        ps_xt = ctx.enter_context(tc.psum_pool(name="ps_xt", bufs=2))
+        keep = ctx.enter_context(tc.tile_pool(name="keep", bufs=NSC))
+        serp = ctx.enter_context(tc.tile_pool(name="serp", bufs=3))
+        msp = ctx.enter_context(tc.tile_pool(name="msp", bufs=3))
+        post = ctx.enter_context(tc.tile_pool(name="post", bufs=5))
+        resp = ctx.enter_context(tc.tile_pool(name="resp", bufs=9))
+        mop = ctx.enter_context(tc.tile_pool(name="mop", bufs=MO_BUFS))
+        ps_tp = ctx.enter_context(tc.psum_pool(name="ps_tp", bufs=4))
         ps_mm = ctx.enter_context(tc.psum_pool(name="ps_mm", bufs=4))
-        ps_ot = ctx.enter_context(tc.psum_pool(name="ps_ot", bufs=2))
         ctx.enter_context(tc.manual_schedule())
 
         x_tiles, gx_t, xt_t, xc_t, mm_t, hidp_t, gh_t, hc_t = {}, {}, {}, {}, {}, {}, {}, {}
-        ser_t, inv_t, ht_t, ot_t, res_t, mod_t = {}, {}, {}, {}, {}, {}
+        ser_t, inv_t, ht_t, ot_t, rs_t, ms_t, mo_t = {}, {}, {}, {}, {}, {}, {}
 
         def live(i):
             return 0 <= i < NSC
 
         def load_x(g):
-            if g * XTA >= NT or g in x_tiles:
+            if g * PAIR >= NT or g in x_tiles:
                 return
-            xr = xin.tile([P, XTA * D], BF16, name="xr")
-            nc.sync.dma_start(out=xr[:], in_=x_view[:, g * XTA * D : (g + 1) * XTA * D])
+            xr = xin.tile([P, PAIR * D], BF16, name="xr")
+            nc.sync.dma_start(out=xr[:], in_=x_view[:, g * PAIR * D : (g + 1) * PAIR * D])
             x_tiles[g] = xr
 
-        def load_mods(i):
-            g = i * SCT // MTA
-            if not live(i) or g in mod_t:
+        def load_ser_mod(g):
+            if g < 0 or g * PAIR >= NT or g in ms_t:
                 return
-            mt = modp.tile([P, NM, MTA, E], BF16, name="mt")
-            for c in range(NM):
-                nc.sync.dma_start(out=mt[:, c, :, :], in_=mod_views[c][:, g * MTA : (g + 1) * MTA, :])
-            mod_t[g] = mt
+            ms = msp.tile([P, PAIR, E], BF16, name="ms")
+            nc.gpsimd.dma_start(out=ms[:], in_=ser_view[:, g * PAIR : (g + 1) * PAIR, :])
+            ms_t[g] = ms
+
+        def load_other_mods(g):
+            if g < 0 or g * PAIR >= NT or g in mo_t:
+                return
+            mo = mop.tile([P, 3, PAIR, E], BF16, name="mo")
+            for k in range(3):
+                nc.gpsimd.dma_start(out=mo[:, k, :, :], in_=other_views[k][:, g * PAIR : (g + 1) * PAIR, :])
+            mo_t[g] = mo
 
         ident = const.tile([P, P], F32)
         make_identity(nc, ident[:])
+        ident_bf = const.tile([P, P], BF16)
+        make_identity(nc, ident_bf[:])
         raw1 = const.tile([P, 4, D], BF16)
         for u in range(2):
             nc.sync.dma_start(
@@ -84,10 +96,10 @@ def tile_hebbianlayer_pb_t_kernel(
                 in_=W1[256 * u : 256 * u + 256, :].rearrange("(q e) f -> q e f", e=2),
             )
         load_x(0)
-        raw2 = const.tile([P, 4, D], BF16)
         b1_bf = const.tile([P, 4], BF16)
         b2_bf = const.tile([P, 4], BF16)
         nc.scalar.dma_start(out=b1_bf[:], in_=b1.rearrange("(m t) -> m t", t=4))
+        raw2 = const.tile([P, 4, D], BF16)
         nc.scalar.dma_start(out=raw2[:], in_=W2.rearrange("(p t) n -> p t n", t=4))
         nc.scalar.dma_start(out=b2_bf[:], in_=b2.rearrange("(j c) -> j c", c=4))
         load_x(1)
@@ -122,11 +134,11 @@ def tile_hebbianlayer_pb_t_kernel(
         def transpose_x(i, h):
             if not live(i):
                 return
-            g, off = divmod(i * SCT, XTA)
+            g, off = divmod(i * SCT, PAIR)
             if off == 0 and h == 0:
                 load_x(g + 1)
             x32 = x_tiles[g][:].bitcast(F32)
-            xt = ps_xt.tile([P, 2, 2, P], F32, name="xt")
+            xt = ps_tp.tile([P, 2, 2, P], F32, name="xt", tag="tp")
             for al in range(2):
                 for u in range(2):
                     col = (off + 2 * h + al) * 256 + u * P
@@ -140,11 +152,9 @@ def tile_hebbianlayer_pb_t_kernel(
                 gx = work.tile([P, 4 * W], BF16, align_bytes=64, name="gx")
                 gx_t[i] = gx
             gx32 = gx_t[i][:].bitcast(F32).rearrange("q (a b u) -> q a b u", a=SCT, u=2)
-            src = xt_t[(i, h)][:].rearrange("q a u b -> q a b u")
-            if False:
-                nc.scalar.copy(out=gx32[:, 2 * h : 2 * h + 2], in_=src)
-            else:
-                nc.vector.tensor_copy(out=gx32[:, 2 * h : 2 * h + 2], in_=src)
+            nc.vector.tensor_copy(
+                out=gx32[:, 2 * h : 2 * h + 2], in_=xt_t[(i, h)][:].rearrange("q a u b -> q a b u")
+            )
 
         def quantise_x(i):
             if not live(i):
@@ -177,12 +187,6 @@ def tile_hebbianlayer_pb_t_kernel(
             if i not in hidp_t:
                 hidp = work.tile([P, 4, W], BF16, name="hidp")
                 hidp_t[i] = hidp
-            if t == 3:
-                nc.vector.tensor_scalar(
-                    out=hidp_t[i][:, t, :], in0=mm_t[(1, i, t)][:], scalar1=b1t[:, t : t + 1], scalar2=0.0,
-                    op0=ALU.add, op1=ALU.max,
-                )
-                return
             nc.scalar.activation(
                 out=hidp_t[i][:, t, :], in_=mm_t[(1, i, t)][:], func=ACT.Relu, bias=b1t[:, t : t + 1], scale=1.0
             )
@@ -200,8 +204,8 @@ def tile_hebbianlayer_pb_t_kernel(
         def quantise_hid(i):
             if not live(i):
                 return
-            hc = hcodes.tile([P, W], U32, align_bytes=64, name="hc")
-            hs = hcodes.tile([P, W], U8, align_bytes=64, name="hs")
+            hc = keep.tile([P, W], U32, align_bytes=64, name="hc")
+            hs = keep.tile([P, W], U8, align_bytes=64, name="hs")
             nc.vector.quantize_mx(
                 out=hc[:].bitcast(FP8X4), scales=hs[:], in_=gh_t[i][:].rearrange("p w t -> p (w t)")
             )
@@ -223,15 +227,50 @@ def tile_hebbianlayer_pb_t_kernel(
         def square_ser(i):
             if not live(i):
                 return
-            inv = serp.tile([P, W], F32, name="inv")
+            inv = keep.tile([P, W], F32, name="inv")
             nc.scalar.activation(out=inv[:], in_=ser_t[i][:], func=ACT.Square)
             inv_t[i] = inv
 
-        def reciprocals(s):
-            last = s - 3
-            if live(last) and last % GROUP == GROUP - 1:
-                for i in range(last - GROUP + 1, last + 1):
-                    nc.scalar.activation(out=inv_t[i][:], in_=inv_t[i][:], func=ACT.Abs_reciprocal_sqrt)
+        def back_to_rows(key, planes, mods, on_pe):
+            bank = ps_tp.tile([P, SCT, E], F32, name="ot", tag="tp")
+            if on_pe:
+                nc.tensor.matmul(out=bank[:], lhsT=ident_bf[:], rhs=mods, start=True, stop=False)
+            for al in range(SCT):
+                src = planes[:, al * P : (al + 1) * P]
+                if on_pe:
+                    nc.tensor.matmul(
+                        out=bank[:, al, :], lhsT=src, rhs=ident[:], is_transpose=True, start=False, stop=(al == SCT - 1)
+                    )
+                else:
+                    nc.tensor.transpose(bank[:, al, :], src, ident[:])
+            ot_t[key] = bank
+
+        def leave_bank(key, mods, on_pe, rows):
+            res = resp.tile([P, SCT, E], F32, name="res")
+            if on_pe:
+                nc.scalar.copy(out=res[:], in_=ot_t[key][:])
+            else:
+                nc.vector.tensor_tensor(out=res[:], in0=ot_t[key][:], in1=mods, op=ALU.add)
+            nc.sync.dma_start(out=rows, in_=res[:])
+
+        def ser_mods(i):
+            g, off = divmod(i * SCT, PAIR)
+            return ms_t[g][:, off : off + SCT, :]
+
+        def other_mods(i, k):
+            g, off = divmod(i * SCT, PAIR)
+            return mo_t[g][:, k, off : off + SCT, :]
+
+        def transpose_ser(i):
+            if live(i):
+                back_to_rows((i, SER), ser_t[i], ser_mods(i), ser_on_scalar(i))
+
+        def exit_ser(i):
+            if live(i):
+                leave_bank((i, SER), ser_mods(i), ser_on_scalar(i), out_view[:, SER, i * SCT : (i + 1) * SCT, :])
+
+        def store_ser(i):
+            return
 
         def layer2(i, n):
             if live(i):
@@ -251,87 +290,85 @@ def tile_hebbianlayer_pb_t_kernel(
         def products(i):
             if not live(i):
                 return
-            nv = 3 - G_PLANES
-            if G_PLANES > 0:
-                nc.gpsimd.tensor_scalar(
-                    out=inv_t[i][:], in0=inv_t[i][:], scalar1=1.0e6, scalar2=0.0, op0=ALU.min, op1=ALU.max
-                )
-                for n in range(nv, 3):
-                    nc.gpsimd.tensor_tensor(out=ht_t[i][:, n, :], in0=ht_t[i][:, n, :], in1=inv_t[i][:], op=ALU.mult)
-            if nv > 0:
-                nc.vector.scalar_tensor_tensor(
-                    out=ht_t[i][:, 0:nv, :],
-                    in0=inv_t[i][:].unsqueeze(1).to_broadcast([P, nv, W]),
-                    scalar=1.0e6,
-                    in1=ht_t[i][:, 0:nv, :],
-                    op0=ALU.min,
-                    op1=ALU.mult,
-                )
-
-        def transpose_back(i, al):
-            if not live(i):
-                return
-            ot = ps_ot.tile([P, NM, E], F32, name="ot")
-            for c in range(NM):
-                if c == SER:
-                    src = ser_t[i][:, al * P : (al + 1) * P]
-                else:
-                    src = ht_t[i][:, OTHERS.index(c), al * P : (al + 1) * P]
-                nc.tensor.transpose(ot[:, c, :], src, ident[:])
-            ot_t[(i, al)] = ot
-
-        def add_modulators(i, al):
-            if not live(i):
-                return
-            if i not in res_t:
-                res = resp.tile([P, NM, SCT, E], F32, name="res")
-                res_t[i] = res
-            g, off = divmod(i * SCT, MTA)
-            nc.vector.tensor_tensor(
-                out=res_t[i][:, :, al, :], in0=ot_t[(i, al)][:], in1=mod_t[g][:, :, off + al, :], op=ALU.add
+            nc.vector.scalar_tensor_tensor(
+                out=ht_t[i][:],
+                in0=inv_t[i][:].unsqueeze(1).to_broadcast([P, 3, W]),
+                scalar=1.0e6,
+                in1=ht_t[i][:],
+                op0=ALU.min,
+                op1=ALU.mult,
             )
 
-        def store(i):
+        def transpose_back(i, k):
             if live(i):
-                nc.sync.dma_start(out=out_view[:, :, i * SCT : (i + 1) * SCT, :], in_=res_t[i][:])
+                back_to_rows((i, OTHERS[k]), ht_t[i][:, k, :], other_mods(i, k), back_on_scalar(i, k))
 
-        for s in range(-1, NSC + LAG + 3 + 1):
-            j = s - LAG
-            load_mods(j + 1)
-            square_ser(s - 3)
-            transpose_back(j - 3, 2)
-            reciprocals(s)
-            transpose_back(j - 3, 3)
-            layer2(j, 0)
-            relu(s - 1, 2)
-            layer2_ser(s - 2)
-            add_modulators(j - 3, 1)
-            layer2(j, 1)
-            add_modulators(j - 3, 0)
-            relu(s - 1, 1)
-            copy_x(s, 1)
-            layer2(j, 2)
-            relu(s - 1, 0)
-            transpose_back(j - 2, 1)
-            relu(s - 1, 3)
-            transpose_x(s + 1, 0)
-            add_modulators(j - 3, 2)
-            tanh(j, 0)
-            tanh_ser(s - 2)
-            transpose_back(j - 2, 0)
-            tanh(j, 1)
-            products(j - 1)
-            add_modulators(j - 3, 3)
+        def exit_back(i, k):
+            if live(i):
+                c = OTHERS[k]
+                leave_bank((i, c), other_mods(i, k), back_on_scalar(i, k), out_view[:, c, i * SCT : (i + 1) * SCT, :])
+
+        for s in range(-1, NSC + 3):
+            load_ser_mod((s - 1) // 2)
+            if s >= 2:
+                load_other_mods(min(MO_BUFS - 1, (s - 2) // 2))
             copy_x(s, 0)
-            store(j - 3)
-            transpose_x(s + 1, 1)
+            copy_x(s, 1)
+            square_ser(s - 3)
+            transpose_ser(s - 3)
+            transpose_x(s + 1, 0)
+            layer2_ser(s - 2)
+            if s - 14 < EARLY:
+                layer2(s - 14, 0)
+            if s - 14 < EARLY:
+                layer2(s - 14, 1)
+            if s - 14 < EARLY:
+                layer2(s - 14, 2)
+            relu(s - 1, 0)
+            relu(s - 1, 1)
+            relu(s - 1, 2)
+            relu(s - 1, 3)
             quantise_x(s)
-            layer1(s, 2)
-            regroup_hid(s - 1)
-            tanh(j, 2)
-            quantise_hid(s - 1)
-            layer1(s, 1)
-            layer1(s, 3)
+            exit_ser(s - 3)
+            store_ser(s - 3)
+            tanh_ser(s - 2)
+            if s - 14 < EARLY:
+                tanh(s - 14, 0)
+            if s - 14 < EARLY:
+                tanh(s - 14, 1)
+            if s - 14 < EARLY:
+                tanh(s - 14, 2)
+            transpose_x(s + 1, 1)
             layer1(s, 0)
+            layer1(s, 1)
+            layer1(s, 2)
+            layer1(s, 3)
+            regroup_hid(s - 1)
+            quantise_hid(s - 1)
             if s == 0:
                 quantise_w2()
+
+        for i in range(NSC):
+            nc.scalar.activation(out=inv_t[i][:], in_=inv_t[i][:], func=ACT.Abs_reciprocal_sqrt)
+
+        for q in range(-2, NSC + 1):
+            load_other_mods((q + 8) // 2)
+            products(q)
+            transpose_back(q - 1, 0)
+            transpose_back(q - 1, 1)
+            transpose_back(q - 1, 2)
+            if q + 2 >= EARLY:
+                layer2(q + 2, 0)
+            if q + 2 >= EARLY:
+                layer2(q + 2, 1)
+            if q + 2 >= EARLY:
+                layer2(q + 2, 2)
+            exit_back(q - 1, 0)
+            exit_back(q - 1, 1)
+            exit_back(q - 1, 2)
+            if q + 2 >= EARLY:
+                tanh(q + 2, 0)
+            if q + 2 >= EARLY:
+                tanh(q + 2, 1)
+            if q + 2 >= EARLY:
+                tanh(q + 2, 2)

@@ -23,10 +23,11 @@ SER = 1
 OTHERS = [0, 2, 3]
 EARLY = 4
 MO_BUFS = 5
+LATE = 13
 
 
 def ser_on_scalar(i):
-    return i % 2 == 1
+    return i % 2 == 1 and i < LATE
 
 
 def back_on_scalar(i, k):
@@ -67,7 +68,13 @@ def tile_hebbianlayer_pb_t_kernel(
             if g * PAIR >= NT or g in x_tiles:
                 return
             xr = xin.tile([P, PAIR * D], BF16, name="xr")
-            nc.sync.dma_start(out=xr[:], in_=x_view[:, g * PAIR * D : (g + 1) * PAIR * D])
+            pieces = 2 if g == 0 else 1
+            width = PAIR * D // pieces
+            for n in range(pieces):
+                nc.sync.dma_start(
+                    out=xr[:, n * width : (n + 1) * width],
+                    in_=x_view[:, g * PAIR * D + n * width : g * PAIR * D + (n + 1) * width],
+                )
             x_tiles[g] = xr
 
         def load_ser_mod(g):
@@ -187,6 +194,12 @@ def tile_hebbianlayer_pb_t_kernel(
             if i not in hidp_t:
                 hidp = work.tile([P, 4, W], BF16, name="hidp")
                 hidp_t[i] = hidp
+            if i >= LATE and t >= 2:
+                nc.vector.tensor_scalar(
+                    out=hidp_t[i][:, t, :], in0=mm_t[(1, i, t)][:], scalar1=b1t[:, t : t + 1], scalar2=0.0,
+                    op0=ALU.add, op1=ALU.max,
+                )
+                return
             nc.scalar.activation(
                 out=hidp_t[i][:, t, :], in_=mm_t[(1, i, t)][:], func=ACT.Relu, bias=b1t[:, t : t + 1], scale=1.0
             )
@@ -318,12 +331,12 @@ def tile_hebbianlayer_pb_t_kernel(
             transpose_ser(s - 3)
             transpose_x(s + 1, 0)
             layer2_ser(s - 2)
-            if s - 14 < EARLY:
-                layer2(s - 14, 0)
-            if s - 14 < EARLY:
-                layer2(s - 14, 1)
-            if s - 14 < EARLY:
-                layer2(s - 14, 2)
+            if s - 13 < EARLY:
+                layer2(s - 13, 0)
+            if s - 13 < EARLY:
+                layer2(s - 13, 1)
+            if s - 13 < EARLY:
+                layer2(s - 13, 2)
             relu(s - 1, 0)
             relu(s - 1, 1)
             relu(s - 1, 2)
@@ -332,12 +345,12 @@ def tile_hebbianlayer_pb_t_kernel(
             exit_ser(s - 3)
             store_ser(s - 3)
             tanh_ser(s - 2)
-            if s - 14 < EARLY:
-                tanh(s - 14, 0)
-            if s - 14 < EARLY:
-                tanh(s - 14, 1)
-            if s - 14 < EARLY:
-                tanh(s - 14, 2)
+            if s - 13 < EARLY:
+                tanh(s - 13, 0)
+            if s - 13 < EARLY:
+                tanh(s - 13, 1)
+            if s - 13 < EARLY:
+                tanh(s - 13, 2)
             transpose_x(s + 1, 1)
             layer1(s, 0)
             layer1(s, 1)

@@ -27,11 +27,11 @@ LATE = 13
 
 
 def ser_on_scalar(i):
-    return i % 2 == 1 and i < LATE
+    return i % 4 != 0 and i < LATE
 
 
 def back_on_scalar(i, k):
-    return i >= EARLY and (k == 2 or (k == 1 and i % 2 == 0))
+    return i >= EARLY and (k == 2 or (k == 1 and i % 3 != 0))
 
 
 def tile_hebbianlayer_pb_t_kernel(

from contextlib import ExitStack

import concourse.mybir as mybir
from concourse.masks import make_identity

F32 = mybir.dt.float32
BF16 = mybir.dt.bfloat16
U32 = mybir.dt.uint32
U8 = mybir.dt.uint8
FP8X4 = mybir.dt.float8_e4m3fn_x4
ACT = mybir.ActivationFunctionType
ALU = mybir.AluOpType

P = 128
B, D, E, NM = 8192, 512, 128, 4
FLOPS = 2 * B * D * D + 2 * B * D * NM * E
NT = B // P
SCT = 4
W = SCT * P
NSC = NT // SCT
PAIR = 2 * SCT
SER = 1
OTHERS = [0, 2, 3]
EARLY = 4
MO_BUFS = 5
LATE = 13


def ser_on_scalar(i):
    return i % 4 != 0 and i < LATE


def back_on_scalar(i, k):
    return i >= EARLY and (k == 2 or (k == 1 and i % 3 != 0))


def tile_hebbianlayer_pb_t_kernel(
    tc, prev_act, W1, b1, W2, b2, dopamine, serotonin, glutamate, gaba, out
):
    nc = tc.nc
    x_view = prev_act.rearrange("(p a) k -> p (a k)", a=NT)
    ser_view = serotonin.rearrange("(p a) j -> p a j", a=NT)
    other_views = [m.rearrange("(p a) j -> p a j", a=NT) for m in (dopamine, glutamate, gaba)]
    out_view = out.rearrange("(c p a) j -> p c a j", c=NM, p=P, a=NT)

    with ExitStack() as ctx:
        const = ctx.enter_context(tc.tile_pool(name="const", bufs=1))
        xin = ctx.enter_context(tc.tile_pool(name="xin", bufs=2))
        work = ctx.enter_context(tc.tile_pool(name="work", bufs=2))
        codes = ctx.enter_context(tc.tile_pool(name="codes", bufs=2))
        keep = ctx.enter_context(tc.tile_pool(name="keep", bufs=NSC))
        serp = ctx.enter_context(tc.tile_pool(name="serp", bufs=3))
        msp = ctx.enter_context(tc.tile_pool(name="msp", bufs=3))
        post = ctx.enter_context(tc.tile_pool(name="post", bufs=5))
        resp = ctx.enter_context(tc.tile_pool(name="resp", bufs=9))
        mop = ctx.enter_context(tc.tile_pool(name="mop", bufs=MO_BUFS))
        ps_tp = ctx.enter_context(tc.psum_pool(name="ps_tp", bufs=4))
        ps_mm = ctx.enter_context(tc.psum_pool(name="ps_mm", bufs=4))
        ctx.enter_context(tc.manual_schedule())

        x_tiles, gx_t, xt_t, xc_t, mm_t, hidp_t, gh_t, hc_t = {}, {}, {}, {}, {}, {}, {}, {}
        ser_t, inv_t, ht_t, ot_t, rs_t, ms_t, mo_t = {}, {}, {}, {}, {}, {}, {}

        def live(i):
            return 0 <= i < NSC

        def load_x(g):
            if g * PAIR >= NT or g in x_tiles:
                return
            xr = xin.tile([P, PAIR * D], BF16, name="xr")
            pieces = 2 if g == 0 else 1
            width = PAIR * D // pieces
            for n in range(pieces):
                nc.sync.dma_start(
                    out=xr[:, n * width : (n + 1) * width],
                    in_=x_view[:, g * PAIR * D + n * width : g * PAIR * D + (n + 1) * width],
                )
            x_tiles[g] = xr

        def load_ser_mod(g):
            if g < 0 or g * PAIR >= NT or g in ms_t:
                return
            ms = msp.tile([P, PAIR, E], BF16, name="ms")
            nc.gpsimd.dma_start(out=ms[:], in_=ser_view[:, g * PAIR : (g + 1) * PAIR, :])
            ms_t[g] = ms

        def load_other_mods(g):
            if g < 0 or g * PAIR >= NT or g in mo_t:
                return
            mo = mop.tile([P, 3, PAIR, E], BF16, name="mo")
            for k in range(3):
                nc.gpsimd.dma_start(out=mo[:, k, :, :], in_=other_views[k][:, g * PAIR : (g + 1) * PAIR, :])
            mo_t[g] = mo

        ident = const.tile([P, P], F32)
        make_identity(nc, ident[:])
        ident_bf = const.tile([P, P], BF16)
        make_identity(nc, ident_bf[:])
        raw1 = const.tile([P, 4, D], BF16)
        for u in range(2):
            nc.sync.dma_start(
                out=raw1[:, 2 * u : 2 * u + 2, :],
                in_=W1[256 * u : 256 * u + 256, :].rearrange("(q e) f -> q e f", e=2),
            )
        load_x(0)
        b1_bf = const.tile([P, 4], BF16)
        b2_bf = const.tile([P, 4], BF16)
        nc.scalar.dma_start(out=b1_bf[:], in_=b1.rearrange("(m t) -> m t", t=4))
        raw2 = const.tile([P, 4, D], BF16)
        nc.scalar.dma_start(out=raw2[:], in_=W2.rearrange("(p t) n -> p t n", t=4))
        nc.scalar.dma_start(out=b2_bf[:], in_=b2.rearrange("(j c) -> j c", c=4))
        load_x(1)

        g1 = const.tile([P, D, 4], BF16, align_bytes=64)
        w1c = const.tile([P, D], U32, align_bytes=64)
        w1s = const.tile([P, D], U8, align_bytes=64)
        nc.vector.tensor_copy(
            out=g1[:].rearrange("q (t m) j -> q t m j", t=4),
            in_=raw1[:].rearrange("q j (m t) -> q t m j", t=4),
        )
        nc.vector.quantize_mx(
            out=w1c[:].bitcast(FP8X4), scales=w1s[:], in_=g1[:].rearrange("q c j -> q (c j)")
        )
        b1t = const.tile([P, 4], F32)
        b2t = const.tile([P, 4], F32)
        nc.vector.tensor_copy(out=b1t[:], in_=b1_bf[:])
        g2 = const.tile([P, D, 4], BF16, align_bytes=64)
        w2c = const.tile([P, D], U32, align_bytes=64)
        w2s = const.tile([P, D], U8, align_bytes=64)
        nc.scalar.copy(
            out=g2[:].rearrange("q (c m) j -> q c m j", c=4),
            in_=raw2[:].rearrange("q j (m c) -> q c m j", c=4),
        )

        def quantise_w2():
            nc.vector.tensor_copy(out=b2t[:], in_=b2_bf[:])
            nc.vector.quantize_mx(
                out=w2c[:].bitcast(FP8X4), scales=w2s[:], in_=g2[:].rearrange("q c j -> q (c j)")
            )

        def transpose_x(i, h):
            if not live(i):
                return
            g, off = divmod(i * SCT, PAIR)
            if off == 0 and h == 0:
                load_x(g + 1)
            x32 = x_tiles[g][:].bitcast(F32)
            xt = ps_tp.tile([P, 2, 2, P], F32, name="xt", tag="tp")
            for al in range(2):
                for u in range(2):
                    col = (off + 2 * h + al) * 256 + u * P
                    nc.tensor.transpose(xt[:, al, u, :], x32[:, col : col + P], ident[:])
            xt_t[(i, h)] = xt

        def copy_x(i, h):
            if not live(i):
                return
            if i not in gx_t:
                gx = work.tile([P, 4 * W], BF16, align_bytes=64, name="gx")
                gx_t[i] = gx
            gx32 = gx_t[i][:].bitcast(F32).rearrange("q (a b u) -> q a b u", a=SCT, u=2)
            nc.vector.tensor_copy(
                out=gx32[:, 2 * h : 2 * h + 2], in_=xt_t[(i, h)][:].rearrange("q a u b -> q a b u")
            )

        def quantise_x(i):
            if not live(i):
                return
            xc = codes.tile([P, W], U32, align_bytes=64, name="xc")
            xs = codes.tile([P, W], U8, align_bytes=64, name="xs")
            nc.vector.quantize_mx(out=xc[:].bitcast(FP8X4), scales=xs[:], in_=gx_t[i][:])
            xc_t[i] = (xc, xs)

        def mx_pass(key, wc, ws, col, operand):
            acc = ps_mm.tile([P, W], F32, name="mm")
            nc.tensor.matmul_mx(
                out=acc[:],
                lhsT=wc[:, col * P : (col + 1) * P].bitcast(FP8X4),
                lhsT_scale=ws[:, col * P : (col + 1) * P],
                rhs=operand[0][:].bitcast(FP8X4),
                rhs_scale=operand[1][:],
                start=True,
                stop=True,
            )
            mm_t[key] = acc

        def layer1(i, t):
            if live(i):
                mx_pass((1, i, t), w1c, w1s, t, xc_t[i])

        def relu(i, t):
            if not live(i):
                return
            if i not in hidp_t:
                hidp = work.tile([P, 4, W], BF16, name="hidp")
                hidp_t[i] = hidp
            if i >= LATE and t >= 2:
                nc.vector.tensor_scalar(
                    out=hidp_t[i][:, t, :], in0=mm_t[(1, i, t)][:], scalar1=b1t[:, t : t + 1], scalar2=0.0,
                    op0=ALU.add, op1=ALU.max,
                )
                return
            nc.scalar.activation(
                out=hidp_t[i][:, t, :], in_=mm_t[(1, i, t)][:], func=ACT.Relu, bias=b1t[:, t : t + 1], scale=1.0
            )

        def regroup_hid(i):
            if not live(i):
                return
            gh = work.tile([P, W, 4], BF16, align_bytes=64, name="gh")
            nc.vector.tensor_copy(
                out=gh[:].rearrange("p (c i) t -> p c t i", i=4),
                in_=hidp_t[i][:].rearrange("p t (c i) -> p c t i", i=4),
            )
            gh_t[i] = gh

        def quantise_hid(i):
            if not live(i):
                return
            hc = keep.tile([P, W], U32, align_bytes=64, name="hc")
            hs = keep.tile([P, W], U8, align_bytes=64, name="hs")
            nc.vector.quantize_mx(
                out=hc[:].bitcast(FP8X4), scales=hs[:], in_=gh_t[i][:].rearrange("p w t -> p (w t)")
            )
            hc_t[i] = (hc, hs)

        def layer2_ser(i):
            if live(i):
                mx_pass((2, i, SER), w2c, w2s, SER, hc_t[i])

        def tanh_ser(i):
            if not live(i):
                return
            ser = serp.tile([P, W], F32, name="ser")
            nc.scalar.activation(
                out=ser[:], in_=mm_t[(2, i, SER)][:], func=ACT.Tanh, bias=b2t[:, SER : SER + 1], scale=1.0
            )
            ser_t[i] = ser

        def square_ser(i):
            if not live(i):
                return
            inv = keep.tile([P, W], F32, name="inv")
            nc.scalar.activation(out=inv[:], in_=ser_t[i][:], func=ACT.Square)
            inv_t[i] = inv

        def back_to_rows(key, planes, mods, on_pe):
            bank = ps_tp.tile([P, SCT, E], F32, name="ot", tag="tp")
            if on_pe:
                nc.tensor.matmul(out=bank[:], lhsT=ident_bf[:], rhs=mods, start=True, stop=False)
            for al in range(SCT):
                src = planes[:, al * P : (al + 1) * P]
                if on_pe:
                    nc.tensor.matmul(
                        out=bank[:, al, :], lhsT=src, rhs=ident[:], is_transpose=True, start=False, stop=(al == SCT - 1)
                    )
                else:
                    nc.tensor.transpose(bank[:, al, :], src, ident[:])
            ot_t[key] = bank

        def leave_bank(key, mods, on_pe, rows):
            res = resp.tile([P, SCT, E], F32, name="res")
            if on_pe:
                nc.scalar.copy(out=res[:], in_=ot_t[key][:])
            else:
                nc.vector.tensor_tensor(out=res[:], in0=ot_t[key][:], in1=mods, op=ALU.add)
            nc.sync.dma_start(out=rows, in_=res[:])

        def ser_mods(i):
            g, off = divmod(i * SCT, PAIR)
            return ms_t[g][:, off : off + SCT, :]

        def other_mods(i, k):
            g, off = divmod(i * SCT, PAIR)
            return mo_t[g][:, k, off : off + SCT, :]

        def transpose_ser(i):
            if live(i):
                back_to_rows((i, SER), ser_t[i], ser_mods(i), ser_on_scalar(i))

        def exit_ser(i):
            if live(i):
                leave_bank((i, SER), ser_mods(i), ser_on_scalar(i), out_view[:, SER, i * SCT : (i + 1) * SCT, :])

        def store_ser(i):
            return

        def layer2(i, n):
            if live(i):
                mx_pass((2, i, OTHERS[n]), w2c, w2s, OTHERS[n], hc_t[i])

        def tanh(i, n):
            if not live(i):
                return
            if i not in ht_t:
                ht = post.tile([P, 3, W], F32, name="ht")
                ht_t[i] = ht
            c = OTHERS[n]
            nc.scalar.activation(
                out=ht_t[i][:, n, :], in_=mm_t[(2, i, c)][:], func=ACT.Tanh, bias=b2t[:, c : c + 1], scale=1.0
            )

        def products(i):
            if not live(i):
                return
            nc.vector.scalar_tensor_tensor(
                out=ht_t[i][:],
                in0=inv_t[i][:].unsqueeze(1).to_broadcast([P, 3, W]),
                scalar=1.0e6,
                in1=ht_t[i][:],
                op0=ALU.min,
                op1=ALU.mult,
            )

        def transpose_back(i, k):
            if live(i):
                back_to_rows((i, OTHERS[k]), ht_t[i][:, k, :], other_mods(i, k), back_on_scalar(i, k))

        def exit_back(i, k):
            if live(i):
                c = OTHERS[k]
                leave_bank((i, c), other_mods(i, k), back_on_scalar(i, k), out_view[:, c, i * SCT : (i + 1) * SCT, :])

        for s in range(-1, NSC + 3):
            load_ser_mod((s - 1) // 2)
            if s >= 2:
                load_other_mods(min(MO_BUFS - 1, (s - 2) // 2))
            copy_x(s, 0)
            copy_x(s, 1)
            square_ser(s - 3)
            transpose_ser(s - 3)
            transpose_x(s + 1, 0)
            layer2_ser(s - 2)
            if s - 13 < EARLY:
                layer2(s - 13, 0)
            if s - 13 < EARLY:
                layer2(s - 13, 1)
            if s - 13 < EARLY:
                layer2(s - 13, 2)
            relu(s - 1, 0)
            relu(s - 1, 1)
            relu(s - 1, 2)
            relu(s - 1, 3)
            quantise_x(s)
            exit_ser(s - 3)
            store_ser(s - 3)
            tanh_ser(s - 2)
            if s - 13 < EARLY:
                tanh(s - 13, 0)
            if s - 13 < EARLY:
                tanh(s - 13, 1)
            if s - 13 < EARLY:
                tanh(s - 13, 2)
            transpose_x(s + 1, 1)
            layer1(s, 0)
            layer1(s, 1)
            layer1(s, 2)
            layer1(s, 3)
            regroup_hid(s - 1)
            quantise_hid(s - 1)
            if s == 0:
                quantise_w2()

        for i in range(NSC):
            nc.scalar.activation(out=inv_t[i][:], in_=inv_t[i][:], func=ACT.Abs_reciprocal_sqrt)

        for q in range(-2, NSC + 1):
            load_other_mods((q + 8) // 2)
            products(q)
            transpose_back(q - 1, 0)
            transpose_back(q - 1, 1)
            transpose_back(q - 1, 2)
            if q + 2 >= EARLY:
                layer2(q + 2, 0)
            if q + 2 >= EARLY:
                layer2(q + 2, 1)
            if q + 2 >= EARLY:
                layer2(q + 2, 2)
            exit_back(q - 1, 0)
            exit_back(q - 1, 1)
            exit_back(q - 1, 2)
            if q + 2 >= EARLY:
                tanh(q + 2, 0)
            if q + 2 >= EARLY:
                tanh(q + 2, 1)
            if q + 2 >= EARLY:
                tanh(q + 2, 2)
